import numpy as np
import ml_dtypes


def mxq(x, axis, fmt="e4m3"):
    dtype, down = {"e4m3": (ml_dtypes.float8_e4m3fn, 7), "e5m2": (ml_dtypes.float8_e5m2, 14)}[fmt]
    v = np.moveaxis(np.asarray(x, np.float32).astype(ml_dtypes.bfloat16).astype(np.float64), axis, -1)
    blocks = v.reshape(v.shape[:-1] + (-1, 32))
    amax = np.abs(blocks).max(-1, keepdims=True)
    byte = np.maximum(np.where(amax > 0, np.frexp(amax)[1] - 1 + 127, 0) - down, 1)
    scale = np.exp2(byte - 127.0)
    codes = (blocks / scale).astype(np.float32).astype(dtype).astype(np.float64)
    return np.moveaxis((codes * scale).reshape(v.shape), -1, axis)


BF16 = ml_dtypes.bfloat16


def bf(x):
    return np.asarray(x, np.float32).astype(BF16)


def f64(x):
    return np.asarray(x).astype(np.float64)


N, M, D = 128, 12288, 512
BANDWIDTHS = (10.0, 512.0)


def multi_rbf(d2):
    return sum(np.exp((-0.5 / b) * d2) for b in BANDWIDTHS)


def setup_inputs():
    u = np.random.standard_normal(D) / np.sqrt(D)
    De = 8.0 * np.random.standard_normal(N)[:, None] * u + 2.0 / np.sqrt(D) * np.random.standard_normal((N, D))
    X = 8.0 * np.random.standard_normal(M)[:, None] * u + 2.0 / np.sqrt(D) * np.random.standard_normal((M, D))
    return {"De": bf(De), "X": bf(X)}


def reference(De, X):
    De, X = f64(De), f64(X)
    Deq = mxq(De, 1, "e4m3")
    sq_de = np.sum(De * De, axis=1)
    xx = Deq @ Deq.T
    dxx = sq_de[:, None] + sq_de[None, :] - 2.0 * xx
    kxx_mean = np.mean(multi_rbf(dxx))

    sq_x = np.sum(X * X, axis=1)
    dxy = sq_x[:, None] + sq_de[None, :] - 2.0 * (mxq(X, 1, "e4m3") @ Deq.T)
    kxy_mean = np.mean(multi_rbf(dxy), axis=1)

    yy_const = float(len(BANDWIDTHS))
    return kxx_mean + yy_const - 2.0 * kxy_mean

@@ -1,0 +1,277 @@
+from contextlib import ExitStack
+
+from concourse import mybir
+from concourse.masks import make_identity
+
+F32 = mybir.dt.float32
+BF16 = mybir.dt.bfloat16
+U32 = mybir.dt.uint32
+U8 = mybir.dt.uint8
+FP8X4 = mybir.dt.float8_e4m3fn_x4
+ALU = mybir.AluOpType
+ACT = mybir.ActivationFunctionType
+AX = mybir.AxisListType
+
+P = 128
+D = 512
+M = 12288
+NT = M // P
+RT = 4
+ROUNDS = NT // RT
+C1 = 0.5 / 10.0
+C2 = 0.5 / 512.0
+CHUNKS = [2,2,2,2,4,4,8,8,8,8,8,8,8,8,8,8]
+FIRST_SLOT = -2
+
+
+def vector_share(r):
+    if r % 3 == 2 and r < ROUNDS - 1:
+        return RT
+    return 2 if r == 0 else 0
+
+
+def ahead_scalar(s):
+    return int(1 + 2.7 * (s - FIRST_SLOT) + 0.5)
+
+
+def ahead_vector(s):
+    return int(1.5 * (s - FIRST_SLOT) + 0.5)
+
+FLOPS = 2 * D * P * (M + P)
+
+
+def tile_filter_t_kernel(tc, De, X, out):
+    nc = tc.nc
+    with ExitStack() as ctx:
+        const = ctx.enter_context(tc.tile_pool(name="const", bufs=1))
+        xpool = ctx.enter_context(tc.tile_pool(name="xpool", bufs=1))
+        gpool = ctx.enter_context(tc.tile_pool(name="gpool", bufs=4))
+        qpool = ctx.enter_context(tc.tile_pool(name="qpool", bufs=4))
+        tpool = ctx.enter_context(tc.tile_pool(name="tpool", bufs=4))
+        jpool = ctx.enter_context(tc.tile_pool(name="jpool", bufs=8))
+        pt_pool = ctx.enter_context(tc.psum_pool(name="pt_pool", bufs=4))
+        ps_pool = ctx.enter_context(tc.psum_pool(name="ps_pool", bufs=3))
+        pm_pool = ctx.enter_context(tc.psum_pool(name="pm_pool", bufs=1))
+        ctx.enter_context(tc.manual_schedule())
+
+        de_sb = const.tile([P, D], BF16, name="de_sb")
+        nc.sync.dma_start(out=de_sb[:], in_=De)
+        xv = X.rearrange("(p t) k -> p t k", t=NT)
+        x_of = []
+        t0 = 0
+        for c, n in enumerate(CHUNKS):
+            xs = xpool.tile([P, n, D], BF16, name="x%d" % c)
+            nc.sync.dma_start(out=xs[:], in_=xv[:, t0 : t0 + n, :])
+            for i in range(n):
+                x_of.append((xs, i))
+            t0 += n
+
+        ident = const.tile([P, P], F32, name="ident")
+        make_identity(nc, ident[:])
+        ones = const.tile([P, P], F32, name="ones")
+        nc.vector.memset(ones[:], 1.0)
+
+        sq_v = const.tile([P, NT], F32, name="sq_v")
+        sq_s = const.tile([P, NT], F32, name="sq_s")
+        nb = const.tile([P, 2, NT], F32, name="nb")
+        s1 = const.tile([P, NT], F32, name="s1")
+        s2 = const.tile([P, NT], F32, name="s2")
+
+        stats = const.tile([P, NT, 6], F32, name="stats")
+        halves = stats[:].rearrange("p t (h c) -> p t h c", c=3)
+
+        def square_norm_s(src, dst):
+            junk = jpool.tile([P, D], BF16, name="sqjunk_s")
+            nc.scalar.activation(out=junk[:], in_=src, func=ACT.Square, accum_out=dst)
+
+        def transpose_tile(src, bank, i):
+            w = src.bitcast(F32)
+            for u in range(2):
+                nc.tensor.transpose(
+                    bank[:, (2 * i + u) * P : (2 * i + u + 1) * P],
+                    w[:, u * P : (u + 1) * P],
+                    ident[:],
+                )
+
+        def exps(t5, bias1, bias2, acc1, acc2):
+            e1 = jpool.tile([P, P], F32, name="e1")
+            nc.scalar.activation(out=e1[:], in_=t5, func=ACT.Exp, bias=bias1, scale=2.0 * C1, accum_out=acc1)
+            e2 = jpool.tile([P, P], F32, name="e2")
+            nc.scalar.activation(out=e2[:], in_=t5, func=ACT.Exp, bias=bias2, scale=2.0 * C2, accum_out=acc2)
+
+        sqde = const.tile([P, 1], F32, name="sqde")
+        square_norm_s(de_sb[:], sqde[:])
+        pde = pm_pool.tile([P, 512], F32, name="pm")
+        transpose_tile(de_sb[:], pde, 0)
+        gde = const.tile([P, D], BF16, name="gde", align_bytes=64)
+        nc.vector.tensor_copy(
+            out=gde[:].bitcast(F32).rearrange("p (m u) -> p m u", u=2),
+            in_=pde[:, 0 : 2 * P].rearrange("p (u m) -> p m u", u=2),
+        )
+        rep = const.tile([P, P], F32, name="rep")
+        nc.vector.tensor_scalar(
+            out=rep[:], in0=ones[:], scalar1=sqde[:, 0:1], scalar2=-0.5, op0=ALU.mult, op1=ALU.mult
+        )
+        de_q = const.tile([P, P], U32, name="de_q", align_bytes=64)
+        de_s = const.tile([P, P], U8, name="de_s", align_bytes=64)
+        nc.vector.quantize_mx(out=de_q[:].bitcast(FP8X4), scales=de_s[:], in_=gde[:])
+        prep = pm_pool.tile([P, 512], F32, name="pm")
+        nc.tensor.transpose(prep[:, 0:P], rep[:], ident[:])
+        hsq4 = const.tile([P, RT, P], F32, name="hsq4")
+        nbde = const.tile([P, 2], F32, name="nbde")
+        txx = const.tile([P, P], F32, name="txx")
+        sxx = const.tile([P, 2], F32, name="sxx")
+        tot = const.tile([P, 1], F32, name="tot")
+        kconst = const.tile([P, 1], F32, name="kconst")
+        xx_state = {}
+
+        def de_late(step):
+            if step == 0:
+                nc.vector.tensor_copy(out=hsq4[:], in_=prep[:, 0:P].unsqueeze(1).to_broadcast([P, RT, P]))
+                nc.vector.tensor_scalar_mul(out=nbde[:, 0:1], in0=sqde[:], scalar1=-C1)
+                nc.vector.tensor_scalar_mul(out=nbde[:, 1:2], in0=sqde[:], scalar1=-C2)
+                pxx = pm_pool.tile([P, 512], F32, name="pm")
+                nc.tensor.matmul_mx(
+                    out=pxx[:, 0:P], lhsT=de_q[:].bitcast(FP8X4), lhsT_scale=de_s[:],
+                    rhs=de_q[:].bitcast(FP8X4), rhs_scale=de_s[:], start=True, stop=True,
+                )
+                xx_state["pxx"] = pxx
+            if step == 1:
+                nc.vector.tensor_tensor(out=txx[:], in0=xx_state["pxx"][:, 0:P], in1=hsq4[:, 0, :], op=ALU.add)
+            if step == 2:
+                exps(txx[:], nbde[:, 0:1], nbde[:, 1:2], sxx[:, 0:1], sxx[:, 1:2])
+            if step == 3:
+                ptot = pm_pool.tile([P, 512], F32, name="pm")
+                nc.tensor.matmul(out=ptot[:, 0:2], lhsT=ones[:], rhs=sxx[:], start=True, stop=True)
+                xx_state["ptot"] = ptot
+            if step == 4:
+                nc.vector.tensor_reduce(out=tot[:], in_=xx_state["ptot"][:, 0:2], axis=AX.X, op=ALU.add)
+                nc.vector.tensor_scalar(
+                    out=kconst[:], in0=tot[:], scalar1=1.0 / (P * P), scalar2=2.0, op0=ALU.mult, op1=ALU.add
+                )
+
+        banks = {}
+        grouped = {}
+        codes = {}
+        sums = {}
+        shifted = {}
+
+        def rng(r):
+            return 0 <= r < ROUNDS
+
+        def transposes(r):
+            for b in range(RT // 2):
+                bank = pt_pool.tile([P, 512], F32, name="pt")
+                for i in range(2):
+                    xs, j = x_of[r * RT + 2 * b + i]
+                    transpose_tile(xs[:, j, :], bank, i)
+                banks[(r, b)] = bank
+
+        def copy_out(r, b):
+            if b == 0:
+                g = gpool.tile([P, RT * D], BF16, name="g", align_bytes=64)
+                grouped[r] = g
+            gw = grouped[r][:].bitcast(F32)
+            nc.vector.tensor_copy(
+                out=gw[:, b * 512 : (b + 1) * 512].rearrange("p (i m u) -> p i m u", i=2, u=2),
+                in_=banks[(r, b)][:].rearrange("p (i u m) -> p i m u", i=2, u=2),
+            )
+
+        def finish_stats(lo, hi):
+            wt = jpool.tile([P, RT, 2], F32, name="wt")
+            w = wt[:, 0 : hi - lo, :]
+            mean = halves[:, lo:hi, :, 1]
+            nc.gpsimd.tensor_tensor(out=w, in0=mean, in1=mean, op=ALU.mult)
+            nc.gpsimd.tensor_scalar(out=w, in0=w, scalar1=D / 2.0, scalar2=0.0, op0=ALU.mult, op1=ALU.add)
+            nc.gpsimd.tensor_tensor(out=w, in0=w, in1=halves[:, lo:hi, :, 2], op=ALU.add)
+            nc.gpsimd.tensor_tensor(out=sq_v[:, lo:hi], in0=w[:, :, 0], in1=w[:, :, 1], op=ALU.add)
+
+        def biases(src, lo, hi):
+            for w, c in enumerate((C1, C2)):
+                nc.gpsimd.tensor_scalar(
+                    out=nb[:, w, lo:hi], in0=src[:, lo:hi], scalar1=-c, scalar2=0.0, op0=ALU.mult, op1=ALU.add
+                )
+
+        def quantise(r):
+            q = qpool.tile([P, RT * P], U32, name="q", align_bytes=64)
+            s = qpool.tile([P, RT * P], U8, name="s", align_bytes=64)
+            nc.vector.quantize_mx(out=q[:].bitcast(FP8X4), scales=s[:], in_=grouped[r][:])
+            codes[r] = (q, s)
+
+        def products(r):
+            q, s = codes[r]
+            ps = ps_pool.tile([P, 512], F32, name="ps")
+            for i in range(RT):
+                cs = slice(i * P, (i + 1) * P)
+                nc.tensor.matmul_mx(
+                    out=ps[:, cs], lhsT=q[:, cs].bitcast(FP8X4), lhsT_scale=s[:, cs],
+                    rhs=de_q[:].bitcast(FP8X4), rhs_scale=de_s[:], start=True, stop=True,
+                )
+            sums[r] = ps
+
+        def shift(r):
+            t5 = tpool.tile([P, RT * P], F32, name="t5")
+            nc.vector.tensor_tensor(
+                out=t5[:], in0=sums[r][:], in1=hsq4[:].rearrange("p i j -> p (i j)"), op=ALU.add
+            )
+            shifted[r] = t5
+
+        def kernels(r):
+            for i in range(RT):
+                t = r * RT + i
+                exps(
+                    shifted[r][:, i * P : (i + 1) * P],
+                    nb[:, 0, t : t + 1], nb[:, 1, t : t + 1], s1[:, t : t + 1], s2[:, t : t + 1],
+                )
+
+        queue_s = []
+        queue_v = []
+        group_of = {}
+        for r in range(ROUNDS):
+            mid = (r + 1) * RT - vector_share(r)
+            queue_s.extend(range(r * RT, mid))
+            queue_v.extend(range(mid, (r + 1) * RT))
+            if mid > r * RT:
+                group_of[mid - 1] = r * RT
+            if vector_share(r) > 0:
+                group_of[(r + 1) * RT - 1] = mid
+        done_s = 0
+        done_v = 0
+        for s in range(FIRST_SLOT, ROUNDS + 3):
+            if rng(s + 1):
+                transposes(s + 1)
+            if rng(s - 2):
+                shift(s - 2)
+            if rng(s - 1):
+                quantise(s - 1)
+                products(s - 1)
+            if rng(s):
+                copy_out(s, 0)
+                copy_out(s, 1)
+            while done_s < min(len(queue_s), ahead_scalar(s)):
+                t = queue_s[done_s]
+                xs, j = x_of[t]
+                square_norm_s(xs[:, j, :], sq_s[:, t : t + 1])
+                if done_s + 1 == len(queue_s) or queue_s[done_s + 1] != t + 1 or (t + 1) % RT == 0:
+                    biases(sq_s, group_of[t], t + 1)
+                done_s += 1
+            while done_v < min(len(queue_v), ahead_vector(s)):
+                t = queue_v[done_v]
+                xs, j = x_of[t]
+                nc.vector.bn_stats(out=stats[:, t, :], in_=xs[:, j, :])
+                if t % RT == RT - 1:
+                    finish_stats(group_of[t], t + 1)
+                    biases(sq_v, group_of[t], t + 1)
+                done_v += 1
+            if rng(s - 3):
+                kernels(s - 3)
+            if 0 <= s <= 4:
+                de_late(s)
+        assert done_s == len(queue_s) and done_v == len(queue_v)
+
+        res = const.tile([P, NT], F32, name="res")
+        nc.vector.tensor_tensor(out=res[:], in0=s1[:], in1=s2[:], op=ALU.add)
+        nc.vector.tensor_scalar(
+            out=res[:], in0=res[:], scalar1=-2.0 / P, scalar2=kconst[:, 0:1], op0=ALU.mult, op1=ALU.add
+        )
+        nc.sync.dma_start(out=out.rearrange("(p t) -> p t", t=NT), in_=res[:])

@@ -24,18 +24,20 @@ CHUNKS = [2,2,2,2,4,4,8,8,8,8,8,8,8,8,8,8]
 FIRST_SLOT = -2
 
 
+def gram_share(r):
+    return 1 if r % 4 == 1 or r % 8 == 4 else 0
+
+
 def vector_share(r):
-    if r % 3 == 2 and r < ROUNDS - 1:
-        return RT
-    return 2 if r == 0 else 0
+    return RT if r % 4 == 2 else 0
 
 
 def ahead_scalar(s):
-    return int(1 + 2.7 * (s - FIRST_SLOT) + 0.5)
+    return int(1 + 2.6 * (s - FIRST_SLOT) + 0.5)
 
 
 def ahead_vector(s):
-    return int(1.5 * (s - FIRST_SLOT) + 0.5)
+    return int(1 + 1.1 * (s - FIRST_SLOT) + 0.5)
 
 FLOPS = 2 * D * P * (M + P)
 
@@ -177,6 +179,24 @@ def tile_filter_t_kernel(tc, De, X, out):
                 in_=banks[(r, b)][:].rearrange("p (i u m) -> p i m u", i=2, u=2),
             )
 
+        grams = {}
+
+        def gram(r):
+            pg = pm_pool.tile([P, 512], F32, name="pm")
+            view = grouped[r][:, 0:D].rearrange("p (m t) -> p t m", t=4)
+            for t in range(4):
+                nc.tensor.matmul(
+                    out=pg[:, 0:P], lhsT=view[:, t, :], rhs=view[:, t, :], start=(t == 0), stop=(t == 3)
+                )
+            grams[r] = pg
+
+        def diagonal(r):
+            junk = jpool.tile([P, P], F32, name="dgjunk")
+            nc.vector.scalar_tensor_tensor(
+                out=junk[:], in0=grams[r][:, 0:P], scalar=1.0, in1=ident[:], op0=ALU.mult, op1=ALU.mult,
+                accum_out=sq_s[:, r * RT : r * RT + 1],
+            )
+
         def finish_stats(lo, hi):
             wt = jpool.tile([P, RT, 2], F32, name="wt")
             w = wt[:, 0 : hi - lo, :]
@@ -229,7 +249,7 @@ def tile_filter_t_kernel(tc, De, X, out):
         group_of = {}
         for r in range(ROUNDS):
             mid = (r + 1) * RT - vector_share(r)
-            queue_s.extend(range(r * RT, mid))
+            queue_s.extend(range(r * RT + gram_share(r), mid))
             queue_v.extend(range(mid, (r + 1) * RT))
             if mid > r * RT:
                 group_of[mid - 1] = r * RT
@@ -242,9 +262,15 @@ def tile_filter_t_kernel(tc, De, X, out):
                 transposes(s + 1)
             if rng(s - 2):
                 shift(s - 2)
+                if gram_share(s - 2):
+                    assert done_s == len(queue_s) or queue_s[done_s] >= (s - 1) * RT
+                    diagonal(s - 2)
+                    biases(sq_s, (s - 2) * RT, (s - 1) * RT)
             if rng(s - 1):
                 quantise(s - 1)
                 products(s - 1)
+                if gram_share(s - 1):
+                    gram(s - 1)
             if rng(s):
                 copy_out(s, 0)
                 copy_out(s, 1)
@@ -252,7 +278,7 @@ def tile_filter_t_kernel(tc, De, X, out):
                 t = queue_s[done_s]
                 xs, j = x_of[t]
                 square_norm_s(xs[:, j, :], sq_s[:, t : t + 1])
-                if done_s + 1 == len(queue_s) or queue_s[done_s + 1] != t + 1 or (t + 1) % RT == 0:
+                if gram_share(t // RT) == 0 and (done_s + 1 == len(queue_s) or queue_s[done_s + 1] != t + 1 or (t + 1) % RT == 0):
                     biases(sq_s, group_of[t], t + 1)
                 done_s += 1
             while done_v < min(len(queue_v), ahead_vector(s)):
@@ -265,8 +291,10 @@ def tile_filter_t_kernel(tc, De, X, out):
                 done_v += 1
             if rng(s - 3):
                 kernels(s - 3)
-            if 0 <= s <= 4:
+            if 0 <= s <= 2:
                 de_late(s)
+            if s in (ROUNDS + 1, ROUNDS + 2):
+                de_late(s - ROUNDS + 2)
         assert done_s == len(queue_s) and done_v == len(queue_v)
 
         res = const.tile([P, NT], F32, name="res")

@@ -25,19 +25,25 @@ FIRST_SLOT = -2
 
 
 def gram_share(r):
-    return 1 if r % 4 == 1 or r % 8 == 4 else 0
+    return 1 if r % 8 in (1, 4, 7) else 0
+
+
+def gpsimd_share(r):
+    return 1 if r > 1 and gram_share(r) == 0 else 0
 
 
 def vector_share(r):
-    return RT if r % 4 == 2 else 0
+    if r == 0:
+        return 2
+    return RT - 1 if r % 6 == 5 else 0
 
 
 def ahead_scalar(s):
-    return int(1 + 2.6 * (s - FIRST_SLOT) + 0.5)
+    return 3 * (s - FIRST_SLOT + 1) if s < 3 else int(15 + 2.2 * (s - 2) + 0.5)
 
 
 def ahead_vector(s):
-    return int(1 + 1.1 * (s - FIRST_SLOT) + 0.5)
+    return int(2 + 0.6 * (s - FIRST_SLOT) + 0.5)
 
 FLOPS = 2 * D * P * (M + P)
 
@@ -50,6 +56,7 @@ def tile_filter_t_kernel(tc, De, X, out):
         gpool = ctx.enter_context(tc.tile_pool(name="gpool", bufs=4))
         qpool = ctx.enter_context(tc.tile_pool(name="qpool", bufs=4))
         tpool = ctx.enter_context(tc.tile_pool(name="tpool", bufs=4))
+        sqpool = ctx.enter_context(tc.tile_pool(name="sqpool", bufs=3))
         jpool = ctx.enter_context(tc.tile_pool(name="jpool", bufs=8))
         pt_pool = ctx.enter_context(tc.psum_pool(name="pt_pool", bufs=4))
         ps_pool = ctx.enter_context(tc.psum_pool(name="ps_pool", bufs=3))
@@ -197,6 +204,28 @@ def tile_filter_t_kernel(tc, De, X, out):
                 accum_out=sq_s[:, r * RT : r * RT + 1],
             )
 
+        squares = {}
+
+        def square_g(r):
+            sq = sqpool.tile([P, 4, P], F32, name="sq")
+            view = grouped[r][:, 0:D].rearrange("p (m t) -> p t m", t=4)
+            nc.gpsimd.tensor_tensor(out=sq[:], in0=view, in1=view, op=ALU.mult)
+            squares[r] = sq
+
+        def turn_g(r):
+            pg = pm_pool.tile([P, 512], F32, name="pm")
+            for t in range(4):
+                nc.tensor.matmul(
+                    out=pg[:, 0:P], lhsT=squares[r][:, t, :], rhs=ident[:], is_transpose=True,
+                    start=(t == 0), stop=(t == 3),
+                )
+            grams[r] = pg
+
+        def sum_g(r):
+            nc.vector.tensor_reduce(
+                out=sq_s[:, r * RT : r * RT + 1], in_=grams[r][:, 0:P], axis=AX.X, op=ALU.add
+            )
+
         def finish_stats(lo, hi):
             wt = jpool.tile([P, RT, 2], F32, name="wt")
             w = wt[:, 0 : hi - lo, :]
@@ -249,10 +278,11 @@ def tile_filter_t_kernel(tc, De, X, out):
         group_of = {}
         for r in range(ROUNDS):
             mid = (r + 1) * RT - vector_share(r)
-            queue_s.extend(range(r * RT + gram_share(r), mid))
+            lo = r * RT + gram_share(r) + gpsimd_share(r)
+            queue_s.extend(range(lo, mid))
             queue_v.extend(range(mid, (r + 1) * RT))
-            if mid > r * RT:
-                group_of[mid - 1] = r * RT
+            if mid > lo:
+                group_of[mid - 1] = lo
             if vector_share(r) > 0:
                 group_of[(r + 1) * RT - 1] = mid
         done_s = 0
@@ -262,23 +292,32 @@ def tile_filter_t_kernel(tc, De, X, out):
                 transposes(s + 1)
             if rng(s - 2):
                 shift(s - 2)
-                if gram_share(s - 2):
-                    assert done_s == len(queue_s) or queue_s[done_s] >= (s - 1) * RT
-                    diagonal(s - 2)
-                    biases(sq_s, (s - 2) * RT, (s - 1) * RT)
+                r = s - 2
+                if gram_share(r) or gpsimd_share(r):
+                    if gram_share(r):
+                        diagonal(r)
+                    else:
+                        sum_g(r)
+                    mid = (r + 1) * RT - vector_share(r)
+                    assert done_s == len(queue_s) or queue_s[done_s] >= mid
+                    biases(sq_s, r * RT, mid)
             if rng(s - 1):
                 quantise(s - 1)
                 products(s - 1)
                 if gram_share(s - 1):
                     gram(s - 1)
+                elif gpsimd_share(s - 1):
+                    turn_g(s - 1)
             if rng(s):
                 copy_out(s, 0)
+                if gpsimd_share(s):
+                    square_g(s)
                 copy_out(s, 1)
             while done_s < min(len(queue_s), ahead_scalar(s)):
                 t = queue_s[done_s]
                 xs, j = x_of[t]
                 square_norm_s(xs[:, j, :], sq_s[:, t : t + 1])
-                if gram_share(t // RT) == 0 and (done_s + 1 == len(queue_s) or queue_s[done_s + 1] != t + 1 or (t + 1) % RT == 0):
+                if gram_share(t // RT) + gpsimd_share(t // RT) == 0 and (done_s + 1 == len(queue_s) or queue_s[done_s + 1] != t + 1 or (t + 1) % RT == 0):
                     biases(sq_s, group_of[t], t + 1)
                 done_s += 1
             while done_v < min(len(queue_v), ahead_vector(s)):

@@ -29,21 +29,21 @@ def gram_share(r):
 
 
 def gpsimd_share(r):
-    return 1 if r > 1 and gram_share(r) == 0 else 0
+    return 1 if r > 0 else 0
 
 
 def vector_share(r):
     if r == 0:
         return 2
-    return RT - 1 if r % 6 == 5 else 0
+    return RT - 1 if r % 8 == 5 else 0
 
 
 def ahead_scalar(s):
-    return 3 * (s - FIRST_SLOT + 1) if s < 3 else int(15 + 2.2 * (s - 2) + 0.5)
+    return 3 * (s - FIRST_SLOT + 1) if s < 3 else int(15 + 1.95 * (s - 2) + 0.5)
 
 
 def ahead_vector(s):
-    return int(2 + 0.6 * (s - FIRST_SLOT) + 0.5)
+    return min(2, s - FIRST_SLOT + 1) if s < 3 else int(2 + 0.5 * (s - 2) + 0.5)
 
 FLOPS = 2 * D * P * (M + P)
 
@@ -56,11 +56,10 @@ def tile_filter_t_kernel(tc, De, X, out):
         gpool = ctx.enter_context(tc.tile_pool(name="gpool", bufs=4))
         qpool = ctx.enter_context(tc.tile_pool(name="qpool", bufs=4))
         tpool = ctx.enter_context(tc.tile_pool(name="tpool", bufs=4))
-        sqpool = ctx.enter_context(tc.tile_pool(name="sqpool", bufs=3))
         jpool = ctx.enter_context(tc.tile_pool(name="jpool", bufs=8))
         pt_pool = ctx.enter_context(tc.psum_pool(name="pt_pool", bufs=4))
-        ps_pool = ctx.enter_context(tc.psum_pool(name="ps_pool", bufs=3))
-        pm_pool = ctx.enter_context(tc.psum_pool(name="pm_pool", bufs=1))
+        ps_pool = ctx.enter_context(tc.psum_pool(name="ps_pool", bufs=2))
+        pm_pool = ctx.enter_context(tc.psum_pool(name="pm_pool", bufs=2))
         ctx.enter_context(tc.manual_schedule())
 
         de_sb = const.tile([P, D], BF16, name="de_sb")
@@ -83,6 +82,9 @@ def tile_filter_t_kernel(tc, De, X, out):
         sq_v = const.tile([P, NT], F32, name="sq_v")
         sq_s = const.tile([P, NT], F32, name="sq_s")
         nb = const.tile([P, 2, NT], F32, name="nb")
+        negc = const.tile([P, 2], F32, name="negc")
+        nc.vector.tensor_scalar_mul(out=negc[:, 0:1], in0=ones[:, 0:1], scalar1=-C1)
+        nc.vector.tensor_scalar_mul(out=negc[:, 1:2], in0=ones[:, 0:1], scalar1=-C2)
         s1 = const.tile([P, NT], F32, name="s1")
         s2 = const.tile([P, NT], F32, name="s2")
 
@@ -190,7 +192,8 @@ def tile_filter_t_kernel(tc, De, X, out):
 
         def gram(r):
             pg = pm_pool.tile([P, 512], F32, name="pm")
-            view = grouped[r][:, 0:D].rearrange("p (m t) -> p t m", t=4)
+            i = gpsimd_share(r)
+            view = grouped[r][:, i * D : (i + 1) * D].rearrange("p (m t) -> p t m", t=4)
             for t in range(4):
                 nc.tensor.matmul(
                     out=pg[:, 0:P], lhsT=view[:, t, :], rhs=view[:, t, :], start=(t == 0), stop=(t == 3)
@@ -198,18 +201,20 @@ def tile_filter_t_kernel(tc, De, X, out):
             grams[r] = pg
 
         def diagonal(r):
+            i = gpsimd_share(r)
             junk = jpool.tile([P, P], F32, name="dgjunk")
             nc.vector.scalar_tensor_tensor(
                 out=junk[:], in0=grams[r][:, 0:P], scalar=1.0, in1=ident[:], op0=ALU.mult, op1=ALU.mult,
-                accum_out=sq_s[:, r * RT : r * RT + 1],
+                accum_out=sq_s[:, r * RT + i : r * RT + i + 1],
             )
 
         squares = {}
+        turned = {}
 
         def square_g(r):
-            sq = sqpool.tile([P, 4, P], F32, name="sq")
+            sq = grouped[r][:].bitcast(F32)[:, D : 2 * D].rearrange("p (t m) -> p t m", t=4)
             view = grouped[r][:, 0:D].rearrange("p (m t) -> p t m", t=4)
-            nc.gpsimd.tensor_tensor(out=sq[:], in0=view, in1=view, op=ALU.mult)
+            nc.gpsimd.tensor_tensor(out=sq, in0=view, in1=view, op=ALU.mult)
             squares[r] = sq
 
         def turn_g(r):
@@ -219,11 +224,11 @@ def tile_filter_t_kernel(tc, De, X, out):
                     out=pg[:, 0:P], lhsT=squares[r][:, t, :], rhs=ident[:], is_transpose=True,
                     start=(t == 0), stop=(t == 3),
                 )
-            grams[r] = pg
+            turned[r] = pg
 
         def sum_g(r):
             nc.vector.tensor_reduce(
-                out=sq_s[:, r * RT : r * RT + 1], in_=grams[r][:, 0:P], axis=AX.X, op=ALU.add
+                out=sq_s[:, r * RT : r * RT + 1], in_=turned[r][:, 0:P], axis=AX.X, op=ALU.add
             )
 
         def finish_stats(lo, hi):
@@ -236,10 +241,11 @@ def tile_filter_t_kernel(tc, De, X, out):
             nc.gpsimd.tensor_tensor(out=sq_v[:, lo:hi], in0=w[:, :, 0], in1=w[:, :, 1], op=ALU.add)
 
         def biases(src, lo, hi):
-            for w, c in enumerate((C1, C2)):
-                nc.gpsimd.tensor_scalar(
-                    out=nb[:, w, lo:hi], in0=src[:, lo:hi], scalar1=-c, scalar2=0.0, op0=ALU.mult, op1=ALU.add
-                )
+            n = hi - lo
+            nc.gpsimd.tensor_tensor(
+                out=nb[:, :, lo:hi], in0=src[:, lo:hi].unsqueeze(1).to_broadcast([P, 2, n]),
+                in1=negc[:].unsqueeze(2).to_broadcast([P, 2, n]), op=ALU.mult,
+            )
 
         def quantise(r):
             q = qpool.tile([P, RT * P], U32, name="q", align_bytes=64)
@@ -292,27 +298,26 @@ def tile_filter_t_kernel(tc, De, X, out):
                 transposes(s + 1)
             if rng(s - 2):
                 shift(s - 2)
-                r = s - 2
-                if gram_share(r) or gpsimd_share(r):
-                    if gram_share(r):
-                        diagonal(r)
-                    else:
-                        sum_g(r)
-                    mid = (r + 1) * RT - vector_share(r)
-                    assert done_s == len(queue_s) or queue_s[done_s] >= mid
-                    biases(sq_s, r * RT, mid)
+                if gram_share(s - 2):
+                    diagonal(s - 2)
+                if gpsimd_share(s - 2):
+                    turn_g(s - 2)
             if rng(s - 1):
                 quantise(s - 1)
+                if gpsimd_share(s - 1):
+                    square_g(s - 1)
                 products(s - 1)
                 if gram_share(s - 1):
                     gram(s - 1)
-                elif gpsimd_share(s - 1):
-                    turn_g(s - 1)
             if rng(s):
                 copy_out(s, 0)
-                if gpsimd_share(s):
-                    square_g(s)
                 copy_out(s, 1)
+            if rng(s - 2) and gram_share(s - 2) + gpsimd_share(s - 2) > 0:
+                if gpsimd_share(s - 2):
+                    sum_g(s - 2)
+                mid = (s - 1) * RT - vector_share(s - 2)
+                assert done_s == len(queue_s) or queue_s[done_s] >= mid
+                biases(sq_s, (s - 2) * RT, mid)
             while done_s < min(len(queue_s), ahead_scalar(s)):
                 t = queue_s[done_s]
                 xs, j = x_of[t]

@@ -25,11 +25,11 @@ FIRST_SLOT = -2
 
 
 def gram_share(r):
-    return 1 if r % 8 in (1, 4, 7) else 0
+    return 1 if r % 8 in (1, 4, 6) else 0
 
 
 def gpsimd_share(r):
-    return 1 if r > 0 else 0
+    return 1 if 0 < r < ROUNDS - 2 else 0
 
 
 def vector_share(r):
@@ -39,7 +39,7 @@ def vector_share(r):
 
 
 def ahead_scalar(s):
-    return 3 * (s - FIRST_SLOT + 1) if s < 3 else int(15 + 1.95 * (s - 2) + 0.5)
+    return 3 * (s - FIRST_SLOT + 1) if s < 3 else int(15 + 2.05 * (s - 2) + 0.5)
 
 
 def ahead_vector(s):
@@ -128,7 +128,7 @@ def tile_filter_t_kernel(tc, De, X, out):
         nc.vector.quantize_mx(out=de_q[:].bitcast(FP8X4), scales=de_s[:], in_=gde[:])
         prep = pm_pool.tile([P, 512], F32, name="pm")
         nc.tensor.transpose(prep[:, 0:P], rep[:], ident[:])
-        hsq4 = const.tile([P, RT, P], F32, name="hsq4")
+        hsq = const.tile([P, P], F32, name="hsq")
         nbde = const.tile([P, 2], F32, name="nbde")
         txx = const.tile([P, P], F32, name="txx")
         sxx = const.tile([P, 2], F32, name="sxx")
@@ -138,7 +138,7 @@ def tile_filter_t_kernel(tc, De, X, out):
 
         def de_late(step):
             if step == 0:
-                nc.vector.tensor_copy(out=hsq4[:], in_=prep[:, 0:P].unsqueeze(1).to_broadcast([P, RT, P]))
+                nc.vector.tensor_copy(out=hsq[:], in_=prep[:, 0:P])
                 nc.vector.tensor_scalar_mul(out=nbde[:, 0:1], in0=sqde[:], scalar1=-C1)
                 nc.vector.tensor_scalar_mul(out=nbde[:, 1:2], in0=sqde[:], scalar1=-C2)
                 pxx = pm_pool.tile([P, 512], F32, name="pm")
@@ -148,7 +148,7 @@ def tile_filter_t_kernel(tc, De, X, out):
                 )
                 xx_state["pxx"] = pxx
             if step == 1:
-                nc.vector.tensor_tensor(out=txx[:], in0=xx_state["pxx"][:, 0:P], in1=hsq4[:, 0, :], op=ALU.add)
+                nc.vector.tensor_tensor(out=txx[:], in0=xx_state["pxx"][:, 0:P], in1=hsq[:], op=ALU.add)
             if step == 2:
                 exps(txx[:], nbde[:, 0:1], nbde[:, 1:2], sxx[:, 0:1], sxx[:, 1:2])
             if step == 3:
@@ -214,7 +214,9 @@ def tile_filter_t_kernel(tc, De, X, out):
         def square_g(r):
             sq = grouped[r][:].bitcast(F32)[:, D : 2 * D].rearrange("p (t m) -> p t m", t=4)
             view = grouped[r][:, 0:D].rearrange("p (m t) -> p t m", t=4)
-            nc.gpsimd.tensor_tensor(out=sq, in0=view, in1=view, op=ALU.mult)
+            for h in range(2):
+                ts = slice(2 * h, 2 * h + 2)
+                nc.gpsimd.tensor_tensor(out=sq[:, ts, :], in0=view[:, ts, :], in1=view[:, ts, :], op=ALU.mult)
             squares[r] = sq
 
         def turn_g(r):
@@ -267,7 +269,8 @@ def tile_filter_t_kernel(tc, De, X, out):
         def shift(r):
             t5 = tpool.tile([P, RT * P], F32, name="t5")
             nc.vector.tensor_tensor(
-                out=t5[:], in0=sums[r][:], in1=hsq4[:].rearrange("p i j -> p (i j)"), op=ALU.add
+                out=t5[:].rearrange("p (i j) -> p i j", i=RT), in0=sums[r][:].rearrange("p (i j) -> p i j", i=RT),
+                in1=hsq[:].unsqueeze(1).to_broadcast([P, RT, P]), op=ALU.add,
             )
             shifted[r] = t5
 

@@ -24,26 +24,37 @@ CHUNKS = [2,2,2,2,4,4,8,8,8,8,8,8,8,8,8,8]
 FIRST_SLOT = -2
 
 
-def gram_share(r):
-    return 1 if r % 8 in (1, 4, 6) else 0
+def on_gpsimd(r):
+    return 0 < r < ROUNDS - 2
 
 
-def gpsimd_share(r):
-    return 1 if 0 < r < ROUNDS - 2 else 0
+def deferred(r):
+    return on_gpsimd(r) and r % 2 == 0
 
 
-def vector_share(r):
+def on_tensor(r):
+    return r % 8 in (1, 3, 5)
+
+
+def maker(r, i):
     if r == 0:
-        return 2
-    return RT - 1 if r % 8 == 5 else 0
+        return "v" if i >= 2 else "s"
+    if i == 0 and on_gpsimd(r):
+        return "g"
+    if i == 3 and deferred(r):
+        return "g"
+    if i == 3 and on_tensor(r):
+        return "t"
+    return "s"
 
 
 def ahead_scalar(s):
-    return 3 * (s - FIRST_SLOT + 1) if s < 3 else int(15 + 2.05 * (s - 2) + 0.5)
+    return 3 * (s - FIRST_SLOT + 1) if s < 3 else int(15 + 2.1 * (s - 2) + 0.5)
 
 
 def ahead_vector(s):
-    return min(2, s - FIRST_SLOT + 1) if s < 3 else int(2 + 0.5 * (s - 2) + 0.5)
+    return s - FIRST_SLOT + 1
+
 
 FLOPS = 2 * D * P * (M + P)
 
@@ -56,6 +67,7 @@ def tile_filter_t_kernel(tc, De, X, out):
         gpool = ctx.enter_context(tc.tile_pool(name="gpool", bufs=4))
         qpool = ctx.enter_context(tc.tile_pool(name="qpool", bufs=4))
         tpool = ctx.enter_context(tc.tile_pool(name="tpool", bufs=4))
+        sqpool = ctx.enter_context(tc.tile_pool(name="sqpool", bufs=2))
         jpool = ctx.enter_context(tc.tile_pool(name="jpool", bufs=8))
         pt_pool = ctx.enter_context(tc.psum_pool(name="pt_pool", bufs=4))
         ps_pool = ctx.enter_context(tc.psum_pool(name="ps_pool", bufs=2))
@@ -104,11 +116,9 @@ def tile_filter_t_kernel(tc, De, X, out):
                     ident[:],
                 )
 
-        def exps(t5, bias1, bias2, acc1, acc2):
-            e1 = jpool.tile([P, P], F32, name="e1")
-            nc.scalar.activation(out=e1[:], in_=t5, func=ACT.Exp, bias=bias1, scale=2.0 * C1, accum_out=acc1)
-            e2 = jpool.tile([P, P], F32, name="e2")
-            nc.scalar.activation(out=e2[:], in_=t5, func=ACT.Exp, bias=bias2, scale=2.0 * C2, accum_out=acc2)
+        def exp_sum(t5, c, bias, acc):
+            e = jpool.tile([P, P], F32, name="e")
+            nc.scalar.activation(out=e[:], in_=t5, func=ACT.Exp, bias=bias, scale=2.0 * c, accum_out=acc)
 
         sqde = const.tile([P, 1], F32, name="sqde")
         square_norm_s(de_sb[:], sqde[:])
@@ -119,15 +129,11 @@ def tile_filter_t_kernel(tc, De, X, out):
             out=gde[:].bitcast(F32).rearrange("p (m u) -> p m u", u=2),
             in_=pde[:, 0 : 2 * P].rearrange("p (u m) -> p m u", u=2),
         )
-        rep = const.tile([P, P], F32, name="rep")
-        nc.vector.tensor_scalar(
-            out=rep[:], in0=ones[:], scalar1=sqde[:, 0:1], scalar2=-0.5, op0=ALU.mult, op1=ALU.mult
-        )
         de_q = const.tile([P, P], U32, name="de_q", align_bytes=64)
         de_s = const.tile([P, P], U8, name="de_s", align_bytes=64)
         nc.vector.quantize_mx(out=de_q[:].bitcast(FP8X4), scales=de_s[:], in_=gde[:])
         prep = pm_pool.tile([P, 512], F32, name="pm")
-        nc.tensor.transpose(prep[:, 0:P], rep[:], ident[:])
+        nc.tensor.transpose(prep[:, 0:P], sqde[:, 0:1].to_broadcast([P, P]), ident[:])
         hsq = const.tile([P, P], F32, name="hsq")
         nbde = const.tile([P, 2], F32, name="nbde")
         txx = const.tile([P, P], F32, name="txx")
@@ -138,9 +144,8 @@ def tile_filter_t_kernel(tc, De, X, out):
 
         def de_late(step):
             if step == 0:
-                nc.vector.tensor_copy(out=hsq[:], in_=prep[:, 0:P])
-                nc.vector.tensor_scalar_mul(out=nbde[:, 0:1], in0=sqde[:], scalar1=-C1)
-                nc.vector.tensor_scalar_mul(out=nbde[:, 1:2], in0=sqde[:], scalar1=-C2)
+                nc.vector.tensor_scalar_mul(out=hsq[:], in0=prep[:, 0:P], scalar1=-0.5)
+                nc.gpsimd.tensor_tensor(out=nbde[:], in0=sqde[:, 0:1].to_broadcast([P, 2]), in1=negc[:], op=ALU.mult)
                 pxx = pm_pool.tile([P, 512], F32, name="pm")
                 nc.tensor.matmul_mx(
                     out=pxx[:, 0:P], lhsT=de_q[:].bitcast(FP8X4), lhsT_scale=de_s[:],
@@ -150,7 +155,8 @@ def tile_filter_t_kernel(tc, De, X, out):
             if step == 1:
                 nc.vector.tensor_tensor(out=txx[:], in0=xx_state["pxx"][:, 0:P], in1=hsq[:], op=ALU.add)
             if step == 2:
-                exps(txx[:], nbde[:, 0:1], nbde[:, 1:2], sxx[:, 0:1], sxx[:, 1:2])
+                for w, c in enumerate((C1, C2)):
+                    exp_sum(txx[:], c, nbde[:, w : w + 1], sxx[:, w : w + 1])
             if step == 3:
                 ptot = pm_pool.tile([P, 512], F32, name="pm")
                 nc.tensor.matmul(out=ptot[:, 0:2], lhsT=ones[:], rhs=sxx[:], start=True, stop=True)
@@ -166,6 +172,10 @@ def tile_filter_t_kernel(tc, De, X, out):
         codes = {}
         sums = {}
         shifted = {}
+        squares = {}
+        late_squares = {}
+        turned = {}
+        grams = {}
 
         def rng(r):
             return 0 <= r < ROUNDS
@@ -188,67 +198,6 @@ def tile_filter_t_kernel(tc, De, X, out):
                 in_=banks[(r, b)][:].rearrange("p (i u m) -> p i m u", i=2, u=2),
             )
 
-        grams = {}
-
-        def gram(r):
-            pg = pm_pool.tile([P, 512], F32, name="pm")
-            i = gpsimd_share(r)
-            view = grouped[r][:, i * D : (i + 1) * D].rearrange("p (m t) -> p t m", t=4)
-            for t in range(4):
-                nc.tensor.matmul(
-                    out=pg[:, 0:P], lhsT=view[:, t, :], rhs=view[:, t, :], start=(t == 0), stop=(t == 3)
-                )
-            grams[r] = pg
-
-        def diagonal(r):
-            i = gpsimd_share(r)
-            junk = jpool.tile([P, P], F32, name="dgjunk")
-            nc.vector.scalar_tensor_tensor(
-                out=junk[:], in0=grams[r][:, 0:P], scalar=1.0, in1=ident[:], op0=ALU.mult, op1=ALU.mult,
-                accum_out=sq_s[:, r * RT + i : r * RT + i + 1],
-            )
-
-        squares = {}
-        turned = {}
-
-        def square_g(r):
-            sq = grouped[r][:].bitcast(F32)[:, D : 2 * D].rearrange("p (t m) -> p t m", t=4)
-            view = grouped[r][:, 0:D].rearrange("p (m t) -> p t m", t=4)
-            for h in range(2):
-                ts = slice(2 * h, 2 * h + 2)
-                nc.gpsimd.tensor_tensor(out=sq[:, ts, :], in0=view[:, ts, :], in1=view[:, ts, :], op=ALU.mult)
-            squares[r] = sq
-
-        def turn_g(r):
-            pg = pm_pool.tile([P, 512], F32, name="pm")
-            for t in range(4):
-                nc.tensor.matmul(
-                    out=pg[:, 0:P], lhsT=squares[r][:, t, :], rhs=ident[:], is_transpose=True,
-                    start=(t == 0), stop=(t == 3),
-                )
-            turned[r] = pg
-
-        def sum_g(r):
-            nc.vector.tensor_reduce(
-                out=sq_s[:, r * RT : r * RT + 1], in_=turned[r][:, 0:P], axis=AX.X, op=ALU.add
-            )
-
-        def finish_stats(lo, hi):
-            wt = jpool.tile([P, RT, 2], F32, name="wt")
-            w = wt[:, 0 : hi - lo, :]
-            mean = halves[:, lo:hi, :, 1]
-            nc.gpsimd.tensor_tensor(out=w, in0=mean, in1=mean, op=ALU.mult)
-            nc.gpsimd.tensor_scalar(out=w, in0=w, scalar1=D / 2.0, scalar2=0.0, op0=ALU.mult, op1=ALU.add)
-            nc.gpsimd.tensor_tensor(out=w, in0=w, in1=halves[:, lo:hi, :, 2], op=ALU.add)
-            nc.gpsimd.tensor_tensor(out=sq_v[:, lo:hi], in0=w[:, :, 0], in1=w[:, :, 1], op=ALU.add)
-
-        def biases(src, lo, hi):
-            n = hi - lo
-            nc.gpsimd.tensor_tensor(
-                out=nb[:, :, lo:hi], in0=src[:, lo:hi].unsqueeze(1).to_broadcast([P, 2, n]),
-                in1=negc[:].unsqueeze(2).to_broadcast([P, 2, n]), op=ALU.mult,
-            )
-
         def quantise(r):
             q = qpool.tile([P, RT * P], U32, name="q", align_bytes=64)
             s = qpool.tile([P, RT * P], U8, name="s", align_bytes=64)
@@ -269,84 +218,164 @@ def tile_filter_t_kernel(tc, De, X, out):
         def shift(r):
             t5 = tpool.tile([P, RT * P], F32, name="t5")
             nc.vector.tensor_tensor(
-                out=t5[:].rearrange("p (i j) -> p i j", i=RT), in0=sums[r][:].rearrange("p (i j) -> p i j", i=RT),
-                in1=hsq[:].unsqueeze(1).to_broadcast([P, RT, P]), op=ALU.add,
+                out=t5[:].rearrange("p (i j) -> p i j", i=RT), in0=hsq[:].unsqueeze(1).to_broadcast([P, RT, P]),
+                in1=sums[r][:].rearrange("p (i j) -> p i j", i=RT), op=ALU.add,
             )
             shifted[r] = t5
 
-        def kernels(r):
-            for i in range(RT):
-                t = r * RT + i
-                exps(
-                    shifted[r][:, i * P : (i + 1) * P],
-                    nb[:, 0, t : t + 1], nb[:, 1, t : t + 1], s1[:, t : t + 1], s2[:, t : t + 1],
-                )
+        def by_element(r, i):
+            return grouped[r][:, i * D : (i + 1) * D].rearrange("p (m t) -> p t m", t=4)
 
-        queue_s = []
-        queue_v = []
-        group_of = {}
-        for r in range(ROUNDS):
-            mid = (r + 1) * RT - vector_share(r)
-            lo = r * RT + gram_share(r) + gpsimd_share(r)
-            queue_s.extend(range(lo, mid))
-            queue_v.extend(range(mid, (r + 1) * RT))
-            if mid > lo:
-                group_of[mid - 1] = lo
-            if vector_share(r) > 0:
-                group_of[(r + 1) * RT - 1] = mid
+        def square_first(r):
+            sq = grouped[r][:].bitcast(F32)[:, D // 2 : D // 2 + D].rearrange("p (t m) -> p t m", t=4)
+            view = by_element(r, 0)
+            nc.gpsimd.tensor_tensor(out=sq, in0=view, in1=view, op=ALU.mult)
+            squares[r] = sq
+
+        def square_late(r, h):
+            if h == 0:
+                sq = sqpool.tile([P, 4, P], F32, name="sq")
+                late_squares[r] = sq
+            ts = slice(2 * h, 2 * h + 2)
+            view = by_element(r, 3)[:, ts, :]
+            nc.gpsimd.tensor_tensor(out=late_squares[r][:, ts, :], in0=view, in1=view, op=ALU.mult)
+
+        def turn(r):
+            pg = pm_pool.tile([P, 512], F32, name="pm")
+            srcs = []
+            if deferred(r - 1):
+                srcs.append(late_squares[r - 1])
+            if on_gpsimd(r):
+                srcs.append(squares[r])
+            for n, sq in enumerate(srcs):
+                for t in range(4):
+                    nc.tensor.matmul(
+                        out=pg[:, n * P : (n + 1) * P], lhsT=sq[:, t, :], rhs=ident[:], is_transpose=True,
+                        start=(t == 0), stop=(t == 3),
+                    )
+            turned[r] = (pg, len(srcs))
+
+        def sum_turned(r):
+            pg, n = turned[r]
+            lo = r * RT - (1 if deferred(r - 1) else 0)
+            nc.vector.tensor_reduce(
+                out=sq_s[:, lo : lo + n], in_=pg[:, 0 : n * P].rearrange("p (n c) -> p n c", n=n),
+                axis=AX.X, op=ALU.add,
+            )
+
+        def gram(r):
+            pg = pm_pool.tile([P, 512], F32, name="pm")
+            view = by_element(r, 3)
+            for t in range(4):
+                nc.tensor.matmul(
+                    out=pg[:, 0:P], lhsT=view[:, t, :], rhs=view[:, t, :], start=(t == 0), stop=(t == 3)
+                )
+            grams[r] = pg
+
+        def diagonal(r):
+            junk = jpool.tile([P, P], F32, name="dgjunk")
+            c = r * RT + 3
+            nc.vector.scalar_tensor_tensor(
+                out=junk[:], in0=ident[:], scalar=1.0, in1=grams[r][:, 0:P], op0=ALU.mult, op1=ALU.mult,
+                accum_out=sq_s[:, c : c + 1],
+            )
+
+        def finish_stats(lo, hi):
+            wt = jpool.tile([P, RT, 2], F32, name="wt")
+            w = wt[:, 0 : hi - lo, :]
+            mean = halves[:, lo:hi, :, 1]
+            nc.gpsimd.tensor_tensor(out=w, in0=mean, in1=mean, op=ALU.mult)
+            nc.gpsimd.tensor_scalar(out=w, in0=w, scalar1=D / 2.0, scalar2=0.0, op0=ALU.mult, op1=ALU.add)
+            nc.gpsimd.tensor_tensor(out=w, in0=w, in1=halves[:, lo:hi, :, 2], op=ALU.add)
+            nc.gpsimd.tensor_tensor(out=sq_v[:, lo:hi], in0=w[:, :, 0], in1=w[:, :, 1], op=ALU.add)
+
+        def biases(src, lo, hi):
+            n = hi - lo
+            nc.gpsimd.tensor_tensor(
+                out=nb[:, :, lo:hi], in0=src[:, lo:hi].unsqueeze(1).to_broadcast([P, 2, n]),
+                in1=negc[:].unsqueeze(2).to_broadcast([P, 2, n]), op=ALU.mult,
+            )
+
+        def ready_tiles(r):
+            first = r * RT - (1 if deferred(r - 1) else 0)
+            last = (r + 1) * RT - (1 if deferred(r) else 0)
+            return range(first, last)
+
+        def round_biases(r):
+            run = []
+            for t in list(ready_tiles(r)) + [None]:
+                if t is not None and maker(t // RT, t % RT) != "v":
+                    run.append(t)
+                elif run:
+                    biases(sq_s, run[0], run[-1] + 1)
+                    run = []
+
+        def kernels(r):
+            for w, (c, acc) in enumerate(((C1, s1), (C2, s2))):
+                for t in ready_tiles(r):
+                    i = t % RT
+                    exp_sum(shifted[t // RT][:, i * P : (i + 1) * P], c, nb[:, w, t : t + 1], acc[:, t : t + 1])
+
+        queue_s = [t for t in range(NT) if maker(t // RT, t % RT) == "s"]
+        queue_v = [t for t in range(NT) if maker(t // RT, t % RT) == "v"]
         done_s = 0
         done_v = 0
         for s in range(FIRST_SLOT, ROUNDS + 3):
             if rng(s + 1):
                 transposes(s + 1)
+            turning = rng(s - 2) and (on_gpsimd(s - 2) or deferred(s - 3))
             if rng(s - 2):
                 shift(s - 2)
-                if gram_share(s - 2):
+                if on_tensor(s - 2):
                     diagonal(s - 2)
-                if gpsimd_share(s - 2):
-                    turn_g(s - 2)
+                if turning:
+                    turn(s - 2)
             if rng(s - 1):
                 quantise(s - 1)
-                if gpsimd_share(s - 1):
-                    square_g(s - 1)
+                if on_gpsimd(s - 1):
+                    square_first(s - 1)
+                if deferred(s - 2):
+                    square_late(s - 2, 1)
+                if deferred(s - 1):
+                    square_late(s - 1, 0)
                 products(s - 1)
-                if gram_share(s - 1):
+                if on_tensor(s - 1):
                     gram(s - 1)
             if rng(s):
                 copy_out(s, 0)
                 copy_out(s, 1)
-            if rng(s - 2) and gram_share(s - 2) + gpsimd_share(s - 2) > 0:
-                if gpsimd_share(s - 2):
-                    sum_g(s - 2)
-                mid = (s - 1) * RT - vector_share(s - 2)
-                assert done_s == len(queue_s) or queue_s[done_s] >= mid
-                biases(sq_s, (s - 2) * RT, mid)
+            if turning:
+                sum_turned(s - 2)
+            if rng(s - 2):
+                assert done_s == len(queue_s) or queue_s[done_s] >= (s - 1) * RT
+                round_biases(s - 2)
             while done_s < min(len(queue_s), ahead_scalar(s)):
                 t = queue_s[done_s]
                 xs, j = x_of[t]
                 square_norm_s(xs[:, j, :], sq_s[:, t : t + 1])
-                if gram_share(t // RT) + gpsimd_share(t // RT) == 0 and (done_s + 1 == len(queue_s) or queue_s[done_s + 1] != t + 1 or (t + 1) % RT == 0):
-                    biases(sq_s, group_of[t], t + 1)
                 done_s += 1
             while done_v < min(len(queue_v), ahead_vector(s)):
                 t = queue_v[done_v]
                 xs, j = x_of[t]
                 nc.vector.bn_stats(out=stats[:, t, :], in_=xs[:, j, :])
-                if t % RT == RT - 1:
-                    finish_stats(group_of[t], t + 1)
-                    biases(sq_v, group_of[t], t + 1)
                 done_v += 1
+                if done_v == len(queue_v) or queue_v[done_v] != t + 1:
+                    finish_stats(t - 1, t + 1)
+                    biases(sq_v, t - 1, t + 1)
             if rng(s - 3):
                 kernels(s - 3)
             if 0 <= s <= 2:
                 de_late(s)
-            if s in (ROUNDS + 1, ROUNDS + 2):
-                de_late(s - ROUNDS + 2)
+            if s in (ROUNDS, ROUNDS + 1):
+                de_late(s - ROUNDS + 3)
         assert done_s == len(queue_s) and done_v == len(queue_v)
 
         res = const.tile([P, NT], F32, name="res")
-        nc.vector.tensor_tensor(out=res[:], in0=s1[:], in1=s2[:], op=ALU.add)
+        part = const.tile([P, NT], F32, name="part")
         nc.vector.tensor_scalar(
-            out=res[:], in0=res[:], scalar1=-2.0 / P, scalar2=kconst[:, 0:1], op0=ALU.mult, op1=ALU.add
+            out=part[:], in0=s1[:], scalar1=-2.0 / P, scalar2=kconst[:, 0:1], op0=ALU.mult, op1=ALU.add
+        )
+        nc.vector.scalar_tensor_tensor(
+            out=res[:], in0=s2[:], scalar=-2.0 / P, in1=part[:], op0=ALU.mult, op1=ALU.add
         )
         nc.sync.dma_start(out=out.rearrange("(p t) -> p t", t=NT), in_=res[:])

@@ -20,7 +20,7 @@ RT = 4
 ROUNDS = NT // RT
 C1 = 0.5 / 10.0
 C2 = 0.5 / 512.0
-CHUNKS = [2,2,2,2,4,4,8,8,8,8,8,8,8,8,8,8]
+CHUNKS = [2] * 4 + [4] * 4 + [8] * 9
 FIRST_SLOT = -2
 
 
@@ -49,7 +49,7 @@ def maker(r, i):
 
 
 def ahead_scalar(s):
-    return 3 * (s - FIRST_SLOT + 1) if s < 3 else int(15 + 2.1 * (s - 2) + 0.5)
+    return 2 * (s - FIRST_SLOT + 1) if s < 3 else int(10 + 2.25 * (s - 2) + 0.5)
 
 
 def ahead_vector(s):
@@ -204,16 +204,26 @@ def tile_filter_t_kernel(tc, De, X, out):
             nc.vector.quantize_mx(out=q[:].bitcast(FP8X4), scales=s[:], in_=grouped[r][:])
             codes[r] = (q, s)
 
+        def open_sums(r):
+            sums[r] = ps_pool.tile([P, 512], F32, name="ps")
+
+        def keep_clock(r):
+            if rng(r - 1):
+                q, s = codes[r - 1]
+                nc.tensor.matmul_mx(
+                    out=sums[r][:], lhsT=de_q[:].bitcast(FP8X4), lhsT_scale=de_s[:],
+                    rhs=q[:].bitcast(FP8X4), rhs_scale=s[:], start=True, stop=True,
+                )
+
         def products(r):
             q, s = codes[r]
-            ps = ps_pool.tile([P, 512], F32, name="ps")
+            ps = sums[r]
             for i in range(RT):
                 cs = slice(i * P, (i + 1) * P)
                 nc.tensor.matmul_mx(
                     out=ps[:, cs], lhsT=q[:, cs].bitcast(FP8X4), lhsT_scale=s[:, cs],
                     rhs=de_q[:].bitcast(FP8X4), rhs_scale=de_s[:], start=True, stop=True,
                 )
-            sums[r] = ps
 
         def shift(r):
             t5 = tpool.tile([P, RT * P], F32, name="t5")
@@ -321,6 +331,9 @@ def tile_filter_t_kernel(tc, De, X, out):
         done_s = 0
         done_v = 0
         for s in range(FIRST_SLOT, ROUNDS + 3):
+            if rng(s - 1):
+                open_sums(s - 1)
+                keep_clock(s - 1)
             if rng(s + 1):
                 transposes(s + 1)
             turning = rng(s - 2) and (on_gpsimd(s - 2) or deferred(s - 3))
@@ -338,6 +351,7 @@ def tile_filter_t_kernel(tc, De, X, out):
                     square_late(s - 2, 1)
                 if deferred(s - 1):
                     square_late(s - 1, 0)
+                keep_clock(s - 1)
                 products(s - 1)
                 if on_tensor(s - 1):
                     gram(s - 1)

@@ -48,6 +48,10 @@ def maker(r, i):
     return "s"
 
 
+def scalar_copies(r):
+    return r % 8 == 4
+
+
 def ahead_scalar(s):
     return 2 * (s - FIRST_SLOT + 1) if s < 3 else int(10 + 2.25 * (s - 2) + 0.5)
 
@@ -193,7 +197,8 @@ def tile_filter_t_kernel(tc, De, X, out):
                 g = gpool.tile([P, RT * D], BF16, name="g", align_bytes=64)
                 grouped[r] = g
             gw = grouped[r][:].bitcast(F32)
-            nc.vector.tensor_copy(
+            copy = nc.scalar.copy if b == 1 and scalar_copies(r) else nc.vector.tensor_copy
+            copy(
                 out=gw[:, b * 512 : (b + 1) * 512].rearrange("p (i m u) -> p i m u", i=2, u=2),
                 in_=banks[(r, b)][:].rearrange("p (i u m) -> p i m u", i=2, u=2),
             )
@@ -204,20 +209,10 @@ def tile_filter_t_kernel(tc, De, X, out):
             nc.vector.quantize_mx(out=q[:].bitcast(FP8X4), scales=s[:], in_=grouped[r][:])
             codes[r] = (q, s)
 
-        def open_sums(r):
-            sums[r] = ps_pool.tile([P, 512], F32, name="ps")
-
-        def keep_clock(r):
-            if rng(r - 1):
-                q, s = codes[r - 1]
-                nc.tensor.matmul_mx(
-                    out=sums[r][:], lhsT=de_q[:].bitcast(FP8X4), lhsT_scale=de_s[:],
-                    rhs=q[:].bitcast(FP8X4), rhs_scale=s[:], start=True, stop=True,
-                )
-
         def products(r):
             q, s = codes[r]
-            ps = sums[r]
+            ps = ps_pool.tile([P, 512], F32, name="ps")
+            sums[r] = ps
             for i in range(RT):
                 cs = slice(i * P, (i + 1) * P)
                 nc.tensor.matmul_mx(
@@ -331,9 +326,6 @@ def tile_filter_t_kernel(tc, De, X, out):
         done_s = 0
         done_v = 0
         for s in range(FIRST_SLOT, ROUNDS + 3):
-            if rng(s - 1):
-                open_sums(s - 1)
-                keep_clock(s - 1)
             if rng(s + 1):
                 transposes(s + 1)
             turning = rng(s - 2) and (on_gpsimd(s - 2) or deferred(s - 3))
@@ -351,7 +343,6 @@ def tile_filter_t_kernel(tc, De, X, out):
                     square_late(s - 2, 1)
                 if deferred(s - 1):
                     square_late(s - 1, 0)
-                keep_clock(s - 1)
                 products(s - 1)
                 if on_tensor(s - 1):
                     gram(s - 1)

from contextlib import ExitStack

from concourse import mybir
from concourse.masks import make_identity

F32 = mybir.dt.float32
BF16 = mybir.dt.bfloat16
U32 = mybir.dt.uint32
U8 = mybir.dt.uint8
FP8X4 = mybir.dt.float8_e4m3fn_x4
ALU = mybir.AluOpType
ACT = mybir.ActivationFunctionType
AX = mybir.AxisListType

P = 128
D = 512
M = 12288
NT = M // P
RT = 4
ROUNDS = NT // RT
C1 = 0.5 / 10.0
C2 = 0.5 / 512.0
CHUNKS = [2] * 4 + [4] * 4 + [8] * 9
FIRST_SLOT = -2


def on_gpsimd(r):
    return 0 < r < ROUNDS - 2


def deferred(r):
    return on_gpsimd(r) and r % 2 == 0


def on_tensor(r):
    return r % 8 in (1, 3, 5)


def maker(r, i):
    if r == 0:
        return "v" if i >= 2 else "s"
    if i == 0 and on_gpsimd(r):
        return "g"
    if i == 3 and deferred(r):
        return "g"
    if i == 3 and on_tensor(r):
        return "t"
    return "s"


def scalar_copies(r):
    return r % 8 == 4


def ahead_scalar(s):
    return 2 * (s - FIRST_SLOT + 1) if s < 3 else int(10 + 2.25 * (s - 2) + 0.5)


def ahead_vector(s):
    return s - FIRST_SLOT + 1


FLOPS = 2 * D * P * (M + P)


def tile_filter_t_kernel(tc, De, X, out):
    nc = tc.nc
    with ExitStack() as ctx:
        const = ctx.enter_context(tc.tile_pool(name="const", bufs=1))
        xpool = ctx.enter_context(tc.tile_pool(name="xpool", bufs=1))
        gpool = ctx.enter_context(tc.tile_pool(name="gpool", bufs=4))
        qpool = ctx.enter_context(tc.tile_pool(name="qpool", bufs=4))
        tpool = ctx.enter_context(tc.tile_pool(name="tpool", bufs=4))
        sqpool = ctx.enter_context(tc.tile_pool(name="sqpool", bufs=2))
        jpool = ctx.enter_context(tc.tile_pool(name="jpool", bufs=8))
        pt_pool = ctx.enter_context(tc.psum_pool(name="pt_pool", bufs=4))
        ps_pool = ctx.enter_context(tc.psum_pool(name="ps_pool", bufs=2))
        pm_pool = ctx.enter_context(tc.psum_pool(name="pm_pool", bufs=2))
        ctx.enter_context(tc.manual_schedule())

        de_sb = const.tile([P, D], BF16, name="de_sb")
        nc.sync.dma_start(out=de_sb[:], in_=De)
        xv = X.rearrange("(p t) k -> p t k", t=NT)
        x_of = []
        t0 = 0
        for c, n in enumerate(CHUNKS):
            xs = xpool.tile([P, n, D], BF16, name="x%d" % c)
            nc.sync.dma_start(out=xs[:], in_=xv[:, t0 : t0 + n, :])
            for i in range(n):
                x_of.append((xs, i))
            t0 += n

        ident = const.tile([P, P], F32, name="ident")
        make_identity(nc, ident[:])
        ones = const.tile([P, P], F32, name="ones")
        nc.vector.memset(ones[:], 1.0)

        sq_v = const.tile([P, NT], F32, name="sq_v")
        sq_s = const.tile([P, NT], F32, name="sq_s")
        nb = const.tile([P, 2, NT], F32, name="nb")
        negc = const.tile([P, 2], F32, name="negc")
        nc.vector.tensor_scalar_mul(out=negc[:, 0:1], in0=ones[:, 0:1], scalar1=-C1)
        nc.vector.tensor_scalar_mul(out=negc[:, 1:2], in0=ones[:, 0:1], scalar1=-C2)
        s1 = const.tile([P, NT], F32, name="s1")
        s2 = const.tile([P, NT], F32, name="s2")

        stats = const.tile([P, NT, 6], F32, name="stats")
        halves = stats[:].rearrange("p t (h c) -> p t h c", c=3)

        def square_norm_s(src, dst):
            junk = jpool.tile([P, D], BF16, name="sqjunk_s")
            nc.scalar.activation(out=junk[:], in_=src, func=ACT.Square, accum_out=dst)

        def transpose_tile(src, bank, i):
            w = src.bitcast(F32)
            for u in range(2):
                nc.tensor.transpose(
                    bank[:, (2 * i + u) * P : (2 * i + u + 1) * P],
                    w[:, u * P : (u + 1) * P],
                    ident[:],
                )

        def exp_sum(t5, c, bias, acc):
            e = jpool.tile([P, P], F32, name="e")
            nc.scalar.activation(out=e[:], in_=t5, func=ACT.Exp, bias=bias, scale=2.0 * c, accum_out=acc)

        sqde = const.tile([P, 1], F32, name="sqde")
        square_norm_s(de_sb[:], sqde[:])
        pde = pm_pool.tile([P, 512], F32, name="pm")
        transpose_tile(de_sb[:], pde, 0)
        gde = const.tile([P, D], BF16, name="gde", align_bytes=64)
        nc.vector.tensor_copy(
            out=gde[:].bitcast(F32).rearrange("p (m u) -> p m u", u=2),
            in_=pde[:, 0 : 2 * P].rearrange("p (u m) -> p m u", u=2),
        )
        de_q = const.tile([P, P], U32, name="de_q", align_bytes=64)
        de_s = const.tile([P, P], U8, name="de_s", align_bytes=64)
        nc.vector.quantize_mx(out=de_q[:].bitcast(FP8X4), scales=de_s[:], in_=gde[:])
        prep = pm_pool.tile([P, 512], F32, name="pm")
        nc.tensor.transpose(prep[:, 0:P], sqde[:, 0:1].to_broadcast([P, P]), ident[:])
        hsq = const.tile([P, P], F32, name="hsq")
        nbde = const.tile([P, 2], F32, name="nbde")
        txx = const.tile([P, P], F32, name="txx")
        sxx = const.tile([P, 2], F32, name="sxx")
        tot = const.tile([P, 1], F32, name="tot")
        kconst = const.tile([P, 1], F32, name="kconst")
        xx_state = {}

        def de_late(step):
            if step == 0:
                nc.vector.tensor_scalar_mul(out=hsq[:], in0=prep[:, 0:P], scalar1=-0.5)
                nc.gpsimd.tensor_tensor(out=nbde[:], in0=sqde[:, 0:1].to_broadcast([P, 2]), in1=negc[:], op=ALU.mult)
                pxx = pm_pool.tile([P, 512], F32, name="pm")
                nc.tensor.matmul_mx(
                    out=pxx[:, 0:P], lhsT=de_q[:].bitcast(FP8X4), lhsT_scale=de_s[:],
                    rhs=de_q[:].bitcast(FP8X4), rhs_scale=de_s[:], start=True, stop=True,
                )
                xx_state["pxx"] = pxx
            if step == 1:
                nc.vector.tensor_tensor(out=txx[:], in0=xx_state["pxx"][:, 0:P], in1=hsq[:], op=ALU.add)
            if step == 2:
                for w, c in enumerate((C1, C2)):
                    exp_sum(txx[:], c, nbde[:, w : w + 1], sxx[:, w : w + 1])
            if step == 3:
                ptot = pm_pool.tile([P, 512], F32, name="pm")
                nc.tensor.matmul(out=ptot[:, 0:2], lhsT=ones[:], rhs=sxx[:], start=True, stop=True)
                xx_state["ptot"] = ptot
            if step == 4:
                nc.vector.tensor_reduce(out=tot[:], in_=xx_state["ptot"][:, 0:2], axis=AX.X, op=ALU.add)
                nc.vector.tensor_scalar(
                    out=kconst[:], in0=tot[:], scalar1=1.0 / (P * P), scalar2=2.0, op0=ALU.mult, op1=ALU.add
                )

        banks = {}
        grouped = {}
        codes = {}
        sums = {}
        shifted = {}
        squares = {}
        late_squares = {}
        turned = {}
        grams = {}

        def rng(r):
            return 0 <= r < ROUNDS

        def transposes(r):
            for b in range(RT // 2):
                bank = pt_pool.tile([P, 512], F32, name="pt")
                for i in range(2):
                    xs, j = x_of[r * RT + 2 * b + i]
                    transpose_tile(xs[:, j, :], bank, i)
                banks[(r, b)] = bank

        def copy_out(r, b):
            if b == 0:
                g = gpool.tile([P, RT * D], BF16, name="g", align_bytes=64)
                grouped[r] = g
            gw = grouped[r][:].bitcast(F32)
            copy = nc.scalar.copy if b == 1 and scalar_copies(r) else nc.vector.tensor_copy
            copy(
                out=gw[:, b * 512 : (b + 1) * 512].rearrange("p (i m u) -> p i m u", i=2, u=2),
                in_=banks[(r, b)][:].rearrange("p (i u m) -> p i m u", i=2, u=2),
            )

        def quantise(r):
            q = qpool.tile([P, RT * P], U32, name="q", align_bytes=64)
            s = qpool.tile([P, RT * P], U8, name="s", align_bytes=64)
            nc.vector.quantize_mx(out=q[:].bitcast(FP8X4), scales=s[:], in_=grouped[r][:])
            codes[r] = (q, s)

        def products(r):
            q, s = codes[r]
            ps = ps_pool.tile([P, 512], F32, name="ps")
            sums[r] = ps
            for i in range(RT):
                cs = slice(i * P, (i + 1) * P)
                nc.tensor.matmul_mx(
                    out=ps[:, cs], lhsT=q[:, cs].bitcast(FP8X4), lhsT_scale=s[:, cs],
                    rhs=de_q[:].bitcast(FP8X4), rhs_scale=de_s[:], start=True, stop=True,
                )

        def shift(r):
            t5 = tpool.tile([P, RT * P], F32, name="t5")
            nc.vector.tensor_tensor(
                out=t5[:].rearrange("p (i j) -> p i j", i=RT), in0=hsq[:].unsqueeze(1).to_broadcast([P, RT, P]),
                in1=sums[r][:].rearrange("p (i j) -> p i j", i=RT), op=ALU.add,
            )
            shifted[r] = t5

        def by_element(r, i):
            return grouped[r][:, i * D : (i + 1) * D].rearrange("p (m t) -> p t m", t=4)

        def square_first(r):
            sq = grouped[r][:].bitcast(F32)[:, D // 2 : D // 2 + D].rearrange("p (t m) -> p t m", t=4)
            view = by_element(r, 0)
            nc.gpsimd.tensor_tensor(out=sq, in0=view, in1=view, op=ALU.mult)
            squares[r] = sq

        def square_late(r, h):
            if h == 0:
                sq = sqpool.tile([P, 4, P], F32, name="sq")
                late_squares[r] = sq
            ts = slice(2 * h, 2 * h + 2)
            view = by_element(r, 3)[:, ts, :]
            nc.gpsimd.tensor_tensor(out=late_squares[r][:, ts, :], in0=view, in1=view, op=ALU.mult)

        def turn(r):
            pg = pm_pool.tile([P, 512], F32, name="pm")
            srcs = []
            if deferred(r - 1):
                srcs.append(late_squares[r - 1])
            if on_gpsimd(r):
                srcs.append(squares[r])
            for n, sq in enumerate(srcs):
                for t in range(4):
                    nc.tensor.matmul(
                        out=pg[:, n * P : (n + 1) * P], lhsT=sq[:, t, :], rhs=ident[:], is_transpose=True,
                        start=(t == 0), stop=(t == 3),
                    )
            turned[r] = (pg, len(srcs))

        def sum_turned(r):
            pg, n = turned[r]
            lo = r * RT - (1 if deferred(r - 1) else 0)
            nc.vector.tensor_reduce(
                out=sq_s[:, lo : lo + n], in_=pg[:, 0 : n * P].rearrange("p (n c) -> p n c", n=n),
                axis=AX.X, op=ALU.add,
            )

        def gram(r):
            pg = pm_pool.tile([P, 512], F32, name="pm")
            view = by_element(r, 3)
            for t in range(4):
                nc.tensor.matmul(
                    out=pg[:, 0:P], lhsT=view[:, t, :], rhs=view[:, t, :], start=(t == 0), stop=(t == 3)
                )
            grams[r] = pg

        def diagonal(r):
            junk = jpool.tile([P, P], F32, name="dgjunk")
            c = r * RT + 3
            nc.vector.scalar_tensor_tensor(
                out=junk[:], in0=ident[:], scalar=1.0, in1=grams[r][:, 0:P], op0=ALU.mult, op1=ALU.mult,
                accum_out=sq_s[:, c : c + 1],
            )

        def finish_stats(lo, hi):
            wt = jpool.tile([P, RT, 2], F32, name="wt")
            w = wt[:, 0 : hi - lo, :]
            mean = halves[:, lo:hi, :, 1]
            nc.gpsimd.tensor_tensor(out=w, in0=mean, in1=mean, op=ALU.mult)
            nc.gpsimd.tensor_scalar(out=w, in0=w, scalar1=D / 2.0, scalar2=0.0, op0=ALU.mult, op1=ALU.add)
            nc.gpsimd.tensor_tensor(out=w, in0=w, in1=halves[:, lo:hi, :, 2], op=ALU.add)
            nc.gpsimd.tensor_tensor(out=sq_v[:, lo:hi], in0=w[:, :, 0], in1=w[:, :, 1], op=ALU.add)

        def biases(src, lo, hi):
            n = hi - lo
            nc.gpsimd.tensor_tensor(
                out=nb[:, :, lo:hi], in0=src[:, lo:hi].unsqueeze(1).to_broadcast([P, 2, n]),
                in1=negc[:].unsqueeze(2).to_broadcast([P, 2, n]), op=ALU.mult,
            )

        def ready_tiles(r):
            first = r * RT - (1 if deferred(r - 1) else 0)
            last = (r + 1) * RT - (1 if deferred(r) else 0)
            return range(first, last)

        def round_biases(r):
            run = []
            for t in list(ready_tiles(r)) + [None]:
                if t is not None and maker(t // RT, t % RT) != "v":
                    run.append(t)
                elif run:
                    biases(sq_s, run[0], run[-1] + 1)
                    run = []

        def kernels(r):
            for w, (c, acc) in enumerate(((C1, s1), (C2, s2))):
                for t in ready_tiles(r):
                    i = t % RT
                    exp_sum(shifted[t // RT][:, i * P : (i + 1) * P], c, nb[:, w, t : t + 1], acc[:, t : t + 1])

        queue_s = [t for t in range(NT) if maker(t // RT, t % RT) == "s"]
        queue_v = [t for t in range(NT) if maker(t // RT, t % RT) == "v"]
        done_s = 0
        done_v = 0
        for s in range(FIRST_SLOT, ROUNDS + 3):
            if rng(s + 1):
                transposes(s + 1)
            turning = rng(s - 2) and (on_gpsimd(s - 2) or deferred(s - 3))
            if rng(s - 2):
                shift(s - 2)
                if on_tensor(s - 2):
                    diagonal(s - 2)
                if turning:
                    turn(s - 2)
            if rng(s - 1):
                quantise(s - 1)
                if on_gpsimd(s - 1):
                    square_first(s - 1)
                if deferred(s - 2):
                    square_late(s - 2, 1)
                if deferred(s - 1):
                    square_late(s - 1, 0)
                products(s - 1)
                if on_tensor(s - 1):
                    gram(s - 1)
            if rng(s):
                copy_out(s, 0)
                copy_out(s, 1)
            if turning:
                sum_turned(s - 2)
            if rng(s - 2):
                assert done_s == len(queue_s) or queue_s[done_s] >= (s - 1) * RT
                round_biases(s - 2)
            while done_s < min(len(queue_s), ahead_scalar(s)):
                t = queue_s[done_s]
                xs, j = x_of[t]
                square_norm_s(xs[:, j, :], sq_s[:, t : t + 1])
                done_s += 1
            while done_v < min(len(queue_v), ahead_vector(s)):
                t = queue_v[done_v]
                xs, j = x_of[t]
                nc.vector.bn_stats(out=stats[:, t, :], in_=xs[:, j, :])
                done_v += 1
                if done_v == len(queue_v) or queue_v[done_v] != t + 1:
                    finish_stats(t - 1, t + 1)
                    biases(sq_v, t - 1, t + 1)
            if rng(s - 3):
                kernels(s - 3)
            if 0 <= s <= 2:
                de_late(s)
            if s in (ROUNDS, ROUNDS + 1):
                de_late(s - ROUNDS + 3)
        assert done_s == len(queue_s) and done_v == len(queue_v)

        res = const.tile([P, NT], F32, name="res")
        part = const.tile([P, NT], F32, name="part")
        nc.vector.tensor_scalar(
            out=part[:], in0=s1[:], scalar1=-2.0 / P, scalar2=kconst[:, 0:1], op0=ALU.mult, op1=ALU.add
        )
        nc.vector.scalar_tensor_tensor(
            out=res[:], in0=s2[:], scalar=-2.0 / P, in1=part[:], op0=ALU.mult, op1=ALU.add
        )
        nc.sync.dma_start(out=out.rearrange("(p t) -> p t", t=NT), in_=res[:])
